import numpy as np
import ml_dtypes


def mxq(x, axis, fmt="e4m3"):
    dtype, down = {"e4m3": (ml_dtypes.float8_e4m3fn, 7), "e5m2": (ml_dtypes.float8_e5m2, 14)}[fmt]
    v = np.moveaxis(np.asarray(x, np.float32).astype(ml_dtypes.bfloat16).astype(np.float64), axis, -1)
    blocks = v.reshape(v.shape[:-1] + (-1, 32))
    amax = np.abs(blocks).max(-1, keepdims=True)
    byte = np.maximum(np.where(amax > 0, np.frexp(amax)[1] - 1 + 127, 0) - down, 1)
    scale = np.exp2(byte - 127.0)
    codes = (blocks / scale).astype(np.float32).astype(dtype).astype(np.float64)
    return np.moveaxis((codes * scale).reshape(v.shape), -1, axis)


WIDE = False


def mx_kscale(k):
    if not WIDE:
        return np.ones(k)
    levels = np.array([10, -10, 5, -5, 0])
    a = np.random.permutation(np.resize(levels, k // 512 * 4)).reshape(k // 512, 4)
    idx = np.arange(k)
    return np.exp2(a[idx // 512, idx % 128 // 32])


BF16 = ml_dtypes.bfloat16


def bf(x):
    return np.asarray(x, np.float32).astype(BF16)


def f64(x):
    return np.asarray(x).astype(np.float64)


B, DIN, H0, H1, L, C, K = 128, 1024, 2048, 1024, 512, 32, 64
BETA = 10.0


def logsumexp(a):
    m = a.max(-1, keepdims=True)
    return (m + np.log(np.exp(a - m).sum(-1, keepdims=True)))[..., 0]


def setup_inputs():
    s, t = mx_kscale(H1), mx_kscale(L)
    return {"h_enc": bf(np.maximum(np.random.standard_normal((B, H1)), 0.0) * s),
            "enc_w2": bf(np.random.standard_normal((H1, L)) * np.sqrt(2.0 / H1) / s[:, None] * t),
            "enc_b2": bf(np.random.standard_normal(L) * 0.1 * t),
            "clus_w": bf(np.random.standard_normal((C, K, L)) * 0.3 / np.sqrt(L) / t),
            "clus_b": bf(np.random.standard_normal((C, K)) * 0.1)}


def reference(h_enc, enc_w2, enc_b2, clus_w, clus_b):
    z = (mxq(f64(h_enc), 1, "e4m3") @ mxq(f64(enc_w2), 0, "e4m3")) + f64(enc_b2)
    wq = mxq(f64(clus_w), 2, "e4m3")
    scores = (mxq(z, 1, "e4m3") @ wq.reshape(C * K, L).T).reshape(B, C, K) + f64(clus_b)
    conf = -logsumexp(-BETA * scores)
    return z, conf

@@ -1,0 +1,241 @@
+from contextlib import ExitStack
+
+import concourse.mybir as mybir
+from concourse.masks import make_identity
+
+F32 = mybir.dt.float32
+BF16 = mybir.dt.bfloat16
+U32 = mybir.dt.uint32
+U8 = mybir.dt.uint8
+FP8X4 = mybir.dt.float8_e4m3fn_x4
+ALU = mybir.AluOpType
+ACT = mybir.ActivationFunctionType
+AXIS = mybir.AxisListType
+
+P = 128
+PACK = 4
+K_PASS = P * PACK
+HIDDEN = 1024
+LATENT = 512
+MODULES = 32
+HEADS = 64
+BETA = 10.0
+
+HIDDEN_PASSES = HIDDEN // K_PASS
+LATENT_TILES = LATENT // P
+CHUNK_ROWS = 512
+CHUNKS = MODULES * HEADS // CHUNK_ROWS
+ROWS_PER_PARTITION = CHUNK_ROWS // P
+CHUNK_MODULES = CHUNK_ROWS // HEADS
+PARTITIONS_PER_MODULE = HEADS // ROWS_PER_PARTITION
+
+FLOPS = 2 * P * HIDDEN * LATENT + 2 * P * LATENT * MODULES * HEADS
+
+
+def tile_ace_pa_s_kernel(tc, h_enc, enc_w2, enc_b2, clus_w, clus_b, z_out, conf_out):
+    nc = tc.nc
+    with ExitStack() as stack:
+        keep = stack.enter_context(tc.tile_pool(name="keep", bufs=1))
+        psum_t = stack.enter_context(tc.psum_pool(name="psum_t", bufs=4))
+        psum_mx = stack.enter_context(tc.psum_pool(name="psum_mx", bufs=4))
+
+        b2_bf16 = keep.tile([P, PACK], BF16)
+        nc.sync.dma_start(
+            out=b2_bf16[:].rearrange("q (u e) -> q u e", e=2),
+            in_=enc_b2.rearrange("(u q e) -> q u e", u=2, e=2),
+        )
+        cb_bf16 = keep.tile([P, CHUNKS, ROWS_PER_PARTITION], BF16)
+        nc.sync.dma_start(
+            out=cb_bf16[:],
+            in_=clus_b.rearrange("c k -> (c k)").rearrange(
+                "(j p r) -> p j r", j=CHUNKS, r=ROWS_PER_PARTITION
+            ),
+        )
+
+        w2_rows = []
+        for g in range(HIDDEN_PASSES):
+            rows = keep.tile([P, PACK, LATENT], BF16, name="w2_rows%d" % g)
+            nc.sync.dma_start(
+                out=rows[:].rearrange("q (u e) d -> q u (e d)", e=2),
+                in_=enc_w2[g * K_PASS : (g + 1) * K_PASS, :].rearrange(
+                    "(u q e) d -> q u (e d)", u=2, e=2
+                ),
+            )
+            w2_rows.append(rows)
+
+        h_rows = keep.tile([P, HIDDEN], BF16)
+        nc.sync.dma_start(out=h_rows[:], in_=h_enc)
+
+        clus_w_rows = clus_w.rearrange("c k d -> (c k) d")
+        cw_rows = []
+        for j in range(CHUNKS):
+            rows = keep.tile([P, ROWS_PER_PARTITION * LATENT], BF16, name="cw_rows%d" % j)
+            nc.sync.dma_start(
+                out=rows[:],
+                in_=clus_w_rows[j * CHUNK_ROWS : (j + 1) * CHUNK_ROWS, :].rearrange(
+                    "(p r) d -> p (r d)", r=ROWS_PER_PARTITION
+                ),
+            )
+            cw_rows.append(rows)
+
+        identity = keep.tile([P, P], F32)
+        make_identity(nc, identity[:])
+        one_column = keep.tile([P, 1], F32)
+        nc.vector.memset(one_column[:], 0.0)
+        table_warmer = keep.tile([P, 1], F32)
+        nc.scalar.activation(out=table_warmer[:], in_=one_column[:], func=ACT.Exp)
+
+        cb_scaled = keep.tile([P, CHUNKS, ROWS_PER_PARTITION], F32)
+        nc.vector.tensor_scalar_mul(out=cb_scaled[:], in0=cb_bf16[:], scalar1=-BETA)
+        bias_rows = []
+        for j in range(CHUNKS):
+            spread = psum_t.tile([P, ROWS_PER_PARTITION, P], F32, tag="t")
+            for r in range(ROWS_PER_PARTITION):
+                nc.tensor.transpose(
+                    spread[:, r, :], cb_scaled[:, j, r : r + 1].to_broadcast([P, P]), identity[:]
+                )
+            rows = keep.tile([P, CHUNK_ROWS], F32, name="bias_rows%d" % j)
+            nc.scalar.copy(out=rows[:], in_=spread[:].rearrange("b r p -> b (r p)"))
+            bias_rows.append(rows)
+
+        w2_grouped = []
+        for g in range(HIDDEN_PASSES):
+            grouped = keep.tile([P, LATENT * PACK], BF16, align_bytes=64, name="w2_grouped%d" % g)
+            nc.vector.tensor_copy(
+                out=grouped[:].rearrange("p (u e q t) -> p u e q t", u=2, e=2, t=PACK),
+                in_=w2_rows[g][:].rearrange("p t (u q e) -> p u e q t", u=2, e=2),
+            )
+            w2_grouped.append(grouped)
+        w2_codes = []
+        w2_scales = []
+        for g in range(HIDDEN_PASSES):
+            codes = keep.tile([P, LATENT], U32, align_bytes=64, name="w2_codes%d" % g)
+            scales = keep.tile([P, LATENT], U8, align_bytes=64, name="w2_scales%d" % g)
+            nc.vector.quantize_mx(out=codes[:].bitcast(FP8X4), scales=scales[:], in_=w2_grouped[g][:])
+            w2_codes.append(codes)
+            w2_scales.append(scales)
+
+        h_words = h_rows[:].bitcast(F32)
+        h_wordsT = psum_t.tile([P, HIDDEN_PASSES, 2, P], F32, tag="t")
+        for g in range(HIDDEN_PASSES):
+            for u in range(2):
+                first = (2 * g + u) * P
+                nc.tensor.transpose(h_wordsT[:, g, u, :], h_words[:, first : first + P], identity[:])
+        h_grouped = keep.tile([P, HIDDEN_PASSES * P * PACK], BF16, align_bytes=64)
+        nc.scalar.copy(
+            out=h_grouped[:].bitcast(F32).rearrange("q (g b u) -> q g b u", g=HIDDEN_PASSES, u=2),
+            in_=h_wordsT[:].rearrange("q g u b -> q g b u"),
+        )
+        h_codes = keep.tile([P, HIDDEN_PASSES * P], U32, align_bytes=64)
+        h_scales = keep.tile([P, HIDDEN_PASSES * P], U8, align_bytes=64)
+        nc.vector.quantize_mx(out=h_codes[:].bitcast(FP8X4), scales=h_scales[:], in_=h_grouped[:])
+
+        zT_sums = psum_mx.tile([P, LATENT_TILES, P], F32, tag="mx")
+        for t in range(LATENT_TILES):
+            for g in range(HIDDEN_PASSES):
+                nc.tensor.matmul_mx(
+                    out=zT_sums[:, t, :],
+                    lhsT=w2_codes[g][:, t * P : (t + 1) * P].bitcast(FP8X4),
+                    lhsT_scale=w2_scales[g][:, t * P : (t + 1) * P],
+                    rhs=h_codes[:, g * P : (g + 1) * P].bitcast(FP8X4),
+                    rhs_scale=h_scales[:, g * P : (g + 1) * P],
+                    start=(g == 0),
+                    stop=(g == HIDDEN_PASSES - 1),
+                )
+
+        b2 = keep.tile([P, PACK], F32)
+        nc.vector.tensor_copy(out=b2[:], in_=b2_bf16[:])
+        z_grouped = keep.tile([P, P * PACK], BF16, align_bytes=64)
+        nc.vector.tensor_tensor(
+            out=z_grouped[:].rearrange("q (b t) -> q b t", t=PACK),
+            in0=zT_sums[:].rearrange("q t b -> q b t"),
+            in1=b2[:].unsqueeze(1).to_broadcast([P, P, PACK]),
+            op=ALU.add,
+        )
+        z_codes = keep.tile([P, P], U32, align_bytes=64)
+        z_scales = keep.tile([P, P], U8, align_bytes=64)
+        nc.vector.quantize_mx(out=z_codes[:].bitcast(FP8X4), scales=z_scales[:], in_=z_grouped[:])
+
+        cw_codes = []
+        cw_scales = []
+        for j in range(CHUNKS):
+            words = cw_rows[j][:].bitcast(F32)
+            grouped = keep.tile([P, CHUNK_ROWS * PACK], BF16, align_bytes=64, name="cw_grouped%d" % j)
+            grouped_words = grouped[:].bitcast(F32).rearrange(
+                "q (r p u) -> q r p u", r=ROWS_PER_PARTITION, u=2
+            )
+            for half in range(2):
+                wordsT = psum_t.tile([P, 2, 2, P], F32, tag="t")
+                for r in range(2):
+                    for u in range(2):
+                        first = ((2 * half + r) * 2 + u) * P
+                        nc.tensor.transpose(wordsT[:, r, u, :], words[:, first : first + P], identity[:])
+                copy_out = nc.scalar.copy if half == 0 else nc.vector.tensor_copy
+                copy_out(
+                    out=grouped_words[:, 2 * half : 2 * half + 2, :, :],
+                    in_=wordsT[:].rearrange("q r u p -> q r p u"),
+                )
+            codes = keep.tile([P, CHUNK_ROWS], U32, align_bytes=64, name="cw_codes%d" % j)
+            scales = keep.tile([P, CHUNK_ROWS], U8, align_bytes=64, name="cw_scales%d" % j)
+            nc.vector.quantize_mx(out=codes[:].bitcast(FP8X4), scales=scales[:], in_=grouped[:])
+            cw_codes.append(codes)
+            cw_scales.append(scales)
+
+        zT = keep.tile([P, LATENT_TILES, P], F32)
+        for t in range(LATENT_TILES):
+            nc.scalar.activation(
+                out=zT[:, t, :], in_=zT_sums[:, t, :], func=ACT.Identity, bias=b2[:, t : t + 1]
+            )
+        z_tiles = psum_t.tile([P, LATENT_TILES, P], F32, tag="t")
+        for t in range(LATENT_TILES):
+            nc.tensor.transpose(z_tiles[:, t, :], zT[:, t, :], identity[:])
+        z_rows = keep.tile([P, LATENT], F32)
+        nc.scalar.copy(
+            out=z_rows[:].rearrange("b (u q e) -> b u q e", u=2, e=2),
+            in_=z_tiles[:].rearrange("b (u e) q -> b u q e", e=2),
+        )
+        nc.sync.dma_start(out=z_out, in_=z_rows[:])
+
+        neg_max = keep.tile([P, MODULES], F32)
+        exp_sum = keep.tile([P, MODULES], F32)
+        for j in range(CHUNKS):
+            sums = psum_mx.tile([P, CHUNK_ROWS], F32, tag="mx")
+            nc.tensor.matmul_mx(
+                out=sums[:],
+                lhsT=z_codes[:].bitcast(FP8X4),
+                lhsT_scale=z_scales[:],
+                rhs=cw_codes[j][:].bitcast(FP8X4),
+                rhs_scale=cw_scales[j][:],
+                start=True,
+                stop=True,
+            )
+            scaled = keep.tile([P, CHUNK_ROWS], F32, name="scaled%d" % j)
+            nc.vector.scalar_tensor_tensor(
+                out=scaled[:], in0=sums[:], scalar=-BETA, in1=bias_rows[j][:], op0=ALU.mult, op1=ALU.add
+            )
+            by_module = scaled[:].rearrange(
+                "b (r m i) -> b m r i", r=ROWS_PER_PARTITION, m=CHUNK_MODULES
+            )
+            modules = slice(j * CHUNK_MODULES, (j + 1) * CHUNK_MODULES)
+            nc.vector.tensor_reduce(
+                out=neg_max[:, modules], in_=by_module, axis=AXIS.XY, op=ALU.max, negate=True
+            )
+            exps = keep.tile([P, CHUNK_ROWS], F32, name="exps%d" % j)
+            exps_by_module = exps[:].rearrange(
+                "b (r m i) -> b m r i", r=ROWS_PER_PARTITION, m=CHUNK_MODULES
+            )
+            for m in range(CHUNK_MODULES):
+                c = j * CHUNK_MODULES + m
+                nc.scalar.activation(
+                    out=exps_by_module[:, m, :, :],
+                    in_=by_module[:, m, :, :],
+                    func=ACT.Exp,
+                    bias=neg_max[:, c : c + 1],
+                    accum_out=exp_sum[:, c : c + 1],
+                )
+
+        log_sum = keep.tile([P, MODULES], F32)
+        nc.scalar.activation(out=log_sum[:], in_=exp_sum[:], func=ACT.Ln)
+        conf = keep.tile([P, MODULES], F32)
+        nc.vector.tensor_sub(out=conf[:], in0=neg_max[:], in1=log_sum[:])
+        nc.sync.dma_start(out=conf_out, in_=conf[:])

@@ -38,6 +38,7 @@ def tile_ace_pa_s_kernel(tc, h_enc, enc_w2, enc_b2, clus_w, clus_b, z_out, conf_
         keep = stack.enter_context(tc.tile_pool(name="keep", bufs=1))
         psum_t = stack.enter_context(tc.psum_pool(name="psum_t", bufs=4))
         psum_mx = stack.enter_context(tc.psum_pool(name="psum_mx", bufs=4))
+        stack.enter_context(tc.manual_schedule())
 
         b2_bf16 = keep.tile([P, PACK], BF16)
         nc.sync.dma_start(
@@ -51,7 +52,6 @@ def tile_ace_pa_s_kernel(tc, h_enc, enc_w2, enc_b2, clus_w, clus_b, z_out, conf_
                 "(j p r) -> p j r", j=CHUNKS, r=ROWS_PER_PARTITION
             ),
         )
-
         w2_rows = []
         for g in range(HIDDEN_PASSES):
             rows = keep.tile([P, PACK, LATENT], BF16, name="w2_rows%d" % g)
@@ -62,10 +62,8 @@ def tile_ace_pa_s_kernel(tc, h_enc, enc_w2, enc_b2, clus_w, clus_b, z_out, conf_
                 ),
             )
             w2_rows.append(rows)
-
         h_rows = keep.tile([P, HIDDEN], BF16)
         nc.sync.dma_start(out=h_rows[:], in_=h_enc)
-
         clus_w_rows = clus_w.rearrange("c k d -> (c k) d")
         cw_rows = []
         for j in range(CHUNKS):
@@ -87,6 +85,8 @@ def tile_ace_pa_s_kernel(tc, h_enc, enc_w2, enc_b2, clus_w, clus_b, z_out, conf_
 
         cb_scaled = keep.tile([P, CHUNKS, ROWS_PER_PARTITION], F32)
         nc.vector.tensor_scalar_mul(out=cb_scaled[:], in0=cb_bf16[:], scalar1=-BETA)
+        b2 = keep.tile([P, PACK], F32)
+        nc.vector.tensor_copy(out=b2[:], in_=b2_bf16[:])
         bias_rows = []
         for j in range(CHUNKS):
             spread = psum_t.tile([P, ROWS_PER_PARTITION, P], F32, tag="t")
@@ -130,6 +130,80 @@ def tile_ace_pa_s_kernel(tc, h_enc, enc_w2, enc_b2, clus_w, clus_b, z_out, conf_
         h_scales = keep.tile([P, HIDDEN_PASSES * P], U8, align_bytes=64)
         nc.vector.quantize_mx(out=h_codes[:].bitcast(FP8X4), scales=h_scales[:], in_=h_grouped[:])
 
+        cw_grouped = [
+            keep.tile([P, CHUNK_ROWS * PACK], BF16, align_bytes=64, name="cw_grouped%d" % j)
+            for j in range(CHUNKS)
+        ]
+        cw_codes = [
+            keep.tile([P, CHUNK_ROWS], U32, align_bytes=64, name="cw_codes%d" % j) for j in range(CHUNKS)
+        ]
+        cw_scales = [
+            keep.tile([P, CHUNK_ROWS], U8, align_bytes=64, name="cw_scales%d" % j) for j in range(CHUNKS)
+        ]
+        scaled = [keep.tile([P, CHUNK_ROWS], F32, name="scaled%d" % j) for j in range(CHUNKS)]
+        neg_max = keep.tile([P, MODULES], F32)
+        exp_sum = keep.tile([P, MODULES], F32)
+
+        def by_module(columns):
+            return columns.rearrange("b (r m i) -> b m r i", r=ROWS_PER_PARTITION, m=CHUNK_MODULES)
+
+        def transpose_chunk(j):
+            words = cw_rows[j][:].bitcast(F32)
+            grouped_words = cw_grouped[j][:].bitcast(F32).rearrange(
+                "q (r p u) -> q r p u", r=ROWS_PER_PARTITION, u=2
+            )
+            for half in range(2):
+                wordsT = psum_t.tile([P, 2, 2, P], F32, tag="t")
+                for r in range(2):
+                    for u in range(2):
+                        first = ((2 * half + r) * 2 + u) * P
+                        nc.tensor.transpose(wordsT[:, r, u, :], words[:, first : first + P], identity[:])
+                nc.scalar.copy(
+                    out=grouped_words[:, 2 * half : 2 * half + 2, :, :],
+                    in_=wordsT[:].rearrange("q r u p -> q r p u"),
+                )
+
+        def quantise_chunk(j):
+            nc.vector.quantize_mx(
+                out=cw_codes[j][:].bitcast(FP8X4), scales=cw_scales[j][:], in_=cw_grouped[j][:]
+            )
+
+        def score_chunk(j):
+            sums = psum_mx.tile([P, CHUNK_ROWS], F32, tag="mx")
+            nc.tensor.matmul_mx(
+                out=sums[:],
+                lhsT=z_codes[:].bitcast(FP8X4),
+                lhsT_scale=z_scales[:],
+                rhs=cw_codes[j][:].bitcast(FP8X4),
+                rhs_scale=cw_scales[j][:],
+                start=True,
+                stop=True,
+            )
+            nc.vector.scalar_tensor_tensor(
+                out=scaled[j][:], in0=sums[:], scalar=-BETA, in1=bias_rows[j][:], op0=ALU.mult, op1=ALU.add
+            )
+            nc.vector.tensor_reduce(
+                out=neg_max[:, j * CHUNK_MODULES : (j + 1) * CHUNK_MODULES],
+                in_=by_module(scaled[j][:]),
+                axis=AXIS.XY,
+                op=ALU.max,
+                negate=True,
+            )
+
+        def sum_exps_chunk(j):
+            exps = keep.tile([P, CHUNK_ROWS], F32, name="exps%d" % j)
+            for m in range(CHUNK_MODULES):
+                c = j * CHUNK_MODULES + m
+                nc.scalar.activation(
+                    out=by_module(exps[:])[:, m, :, :],
+                    in_=by_module(scaled[j][:])[:, m, :, :],
+                    func=ACT.Exp,
+                    bias=neg_max[:, c : c + 1],
+                    accum_out=exp_sum[:, c : c + 1],
+                )
+
+        transpose_chunk(0)
+
         zT_sums = psum_mx.tile([P, LATENT_TILES, P], F32, tag="mx")
         for t in range(LATENT_TILES):
             for g in range(HIDDEN_PASSES):
@@ -143,8 +217,9 @@ def tile_ace_pa_s_kernel(tc, h_enc, enc_w2, enc_b2, clus_w, clus_b, z_out, conf_
                     stop=(g == HIDDEN_PASSES - 1),
                 )
 
-        b2 = keep.tile([P, PACK], F32)
-        nc.vector.tensor_copy(out=b2[:], in_=b2_bf16[:])
+        transpose_chunk(1)
+        quantise_chunk(0)
+
         z_grouped = keep.tile([P, P * PACK], BF16, align_bytes=64)
         nc.vector.tensor_tensor(
             out=z_grouped[:].rearrange("q (b t) -> q b t", t=PACK),
@@ -155,84 +230,33 @@ def tile_ace_pa_s_kernel(tc, h_enc, enc_w2, enc_b2, clus_w, clus_b, z_out, conf_
         z_codes = keep.tile([P, P], U32, align_bytes=64)
         z_scales = keep.tile([P, P], U8, align_bytes=64)
         nc.vector.quantize_mx(out=z_codes[:].bitcast(FP8X4), scales=z_scales[:], in_=z_grouped[:])
-
-        cw_codes = []
-        cw_scales = []
-        for j in range(CHUNKS):
-            words = cw_rows[j][:].bitcast(F32)
-            grouped = keep.tile([P, CHUNK_ROWS * PACK], BF16, align_bytes=64, name="cw_grouped%d" % j)
-            grouped_words = grouped[:].bitcast(F32).rearrange(
-                "q (r p u) -> q r p u", r=ROWS_PER_PARTITION, u=2
-            )
-            for half in range(2):
-                wordsT = psum_t.tile([P, 2, 2, P], F32, tag="t")
-                for r in range(2):
-                    for u in range(2):
-                        first = ((2 * half + r) * 2 + u) * P
-                        nc.tensor.transpose(wordsT[:, r, u, :], words[:, first : first + P], identity[:])
-                copy_out = nc.scalar.copy if half == 0 else nc.vector.tensor_copy
-                copy_out(
-                    out=grouped_words[:, 2 * half : 2 * half + 2, :, :],
-                    in_=wordsT[:].rearrange("q r u p -> q r p u"),
-                )
-            codes = keep.tile([P, CHUNK_ROWS], U32, align_bytes=64, name="cw_codes%d" % j)
-            scales = keep.tile([P, CHUNK_ROWS], U8, align_bytes=64, name="cw_scales%d" % j)
-            nc.vector.quantize_mx(out=codes[:].bitcast(FP8X4), scales=scales[:], in_=grouped[:])
-            cw_codes.append(codes)
-            cw_scales.append(scales)
+        quantise_chunk(1)
 
         zT = keep.tile([P, LATENT_TILES, P], F32)
         for t in range(LATENT_TILES):
             nc.scalar.activation(
                 out=zT[:, t, :], in_=zT_sums[:, t, :], func=ACT.Identity, bias=b2[:, t : t + 1]
             )
-        z_tiles = psum_t.tile([P, LATENT_TILES, P], F32, tag="t")
-        for t in range(LATENT_TILES):
-            nc.tensor.transpose(z_tiles[:, t, :], zT[:, t, :], identity[:])
-        z_rows = keep.tile([P, LATENT], F32)
-        nc.scalar.copy(
-            out=z_rows[:].rearrange("b (u q e) -> b u q e", u=2, e=2),
-            in_=z_tiles[:].rearrange("b (u e) q -> b u q e", e=2),
-        )
-        nc.sync.dma_start(out=z_out, in_=z_rows[:])
 
-        neg_max = keep.tile([P, MODULES], F32)
-        exp_sum = keep.tile([P, MODULES], F32)
         for j in range(CHUNKS):
-            sums = psum_mx.tile([P, CHUNK_ROWS], F32, tag="mx")
-            nc.tensor.matmul_mx(
-                out=sums[:],
-                lhsT=z_codes[:].bitcast(FP8X4),
-                lhsT_scale=z_scales[:],
-                rhs=cw_codes[j][:].bitcast(FP8X4),
-                rhs_scale=cw_scales[j][:],
-                start=True,
-                stop=True,
-            )
-            scaled = keep.tile([P, CHUNK_ROWS], F32, name="scaled%d" % j)
-            nc.vector.scalar_tensor_tensor(
-                out=scaled[:], in0=sums[:], scalar=-BETA, in1=bias_rows[j][:], op0=ALU.mult, op1=ALU.add
-            )
-            by_module = scaled[:].rearrange(
-                "b (r m i) -> b m r i", r=ROWS_PER_PARTITION, m=CHUNK_MODULES
-            )
-            modules = slice(j * CHUNK_MODULES, (j + 1) * CHUNK_MODULES)
-            nc.vector.tensor_reduce(
-                out=neg_max[:, modules], in_=by_module, axis=AXIS.XY, op=ALU.max, negate=True
-            )
-            exps = keep.tile([P, CHUNK_ROWS], F32, name="exps%d" % j)
-            exps_by_module = exps[:].rearrange(
-                "b (r m i) -> b m r i", r=ROWS_PER_PARTITION, m=CHUNK_MODULES
-            )
-            for m in range(CHUNK_MODULES):
-                c = j * CHUNK_MODULES + m
-                nc.scalar.activation(
-                    out=exps_by_module[:, m, :, :],
-                    in_=by_module[:, m, :, :],
-                    func=ACT.Exp,
-                    bias=neg_max[:, c : c + 1],
-                    accum_out=exp_sum[:, c : c + 1],
+            if j + 2 < CHUNKS:
+                transpose_chunk(j + 2)
+            score_chunk(j)
+            if j + 2 < CHUNKS:
+                quantise_chunk(j + 2)
+            if j >= 1:
+                sum_exps_chunk(j - 1)
+            if j == 1:
+                z_tiles = psum_t.tile([P, LATENT_TILES, P], F32, tag="t")
+                for t in range(LATENT_TILES):
+                    nc.tensor.transpose(z_tiles[:, t, :], zT[:, t, :], identity[:])
+                z_rows = keep.tile([P, LATENT], F32)
+                nc.scalar.copy(
+                    out=z_rows[:].rearrange("b (u q e) -> b u q e", u=2, e=2),
+                    in_=z_tiles[:].rearrange("b (u e) q -> b u q e", e=2),
                 )
+                nc.sync.dma_start(out=z_out, in_=z_rows[:])
+        sum_exps_chunk(CHUNKS - 1)
 
         log_sum = keep.tile([P, MODULES], F32)
         nc.scalar.activation(out=log_sum[:], in_=exp_sum[:], func=ACT.Ln)

@@ -27,7 +27,7 @@ CHUNK_ROWS = 512
 CHUNKS = MODULES * HEADS // CHUNK_ROWS
 ROWS_PER_PARTITION = CHUNK_ROWS // P
 CHUNK_MODULES = CHUNK_ROWS // HEADS
-PARTITIONS_PER_MODULE = HEADS // ROWS_PER_PARTITION
+GROUP_MODULES = CHUNK_MODULES // 2
 
 FLOPS = 2 * P * HIDDEN * LATENT + 2 * P * LATENT * MODULES * HEADS
 
@@ -40,11 +40,6 @@ def tile_ace_pa_s_kernel(tc, h_enc, enc_w2, enc_b2, clus_w, clus_b, z_out, conf_
         psum_mx = stack.enter_context(tc.psum_pool(name="psum_mx", bufs=4))
         stack.enter_context(tc.manual_schedule())
 
-        b2_bf16 = keep.tile([P, PACK], BF16)
-        nc.sync.dma_start(
-            out=b2_bf16[:].rearrange("q (u e) -> q u e", e=2),
-            in_=enc_b2.rearrange("(u q e) -> q u e", u=2, e=2),
-        )
         cb_bf16 = keep.tile([P, CHUNKS, ROWS_PER_PARTITION], BF16)
         nc.sync.dma_start(
             out=cb_bf16[:],
@@ -64,6 +59,11 @@ def tile_ace_pa_s_kernel(tc, h_enc, enc_w2, enc_b2, clus_w, clus_b, z_out, conf_
             w2_rows.append(rows)
         h_rows = keep.tile([P, HIDDEN], BF16)
         nc.sync.dma_start(out=h_rows[:], in_=h_enc)
+        b2_bf16 = keep.tile([P, PACK], BF16)
+        nc.sync.dma_start(
+            out=b2_bf16[:].rearrange("q (u e) -> q u e", e=2),
+            in_=enc_b2.rearrange("(u q e) -> q u e", u=2, e=2),
+        )
         clus_w_rows = clus_w.rearrange("c k d -> (c k) d")
         cw_rows = []
         for j in range(CHUNKS):
@@ -85,8 +85,6 @@ def tile_ace_pa_s_kernel(tc, h_enc, enc_w2, enc_b2, clus_w, clus_b, z_out, conf_
 
         cb_scaled = keep.tile([P, CHUNKS, ROWS_PER_PARTITION], F32)
         nc.vector.tensor_scalar_mul(out=cb_scaled[:], in0=cb_bf16[:], scalar1=-BETA)
-        b2 = keep.tile([P, PACK], F32)
-        nc.vector.tensor_copy(out=b2[:], in_=b2_bf16[:])
         bias_rows = []
         for j in range(CHUNKS):
             spread = psum_t.tile([P, ROWS_PER_PARTITION, P], F32, tag="t")
@@ -126,6 +124,8 @@ def tile_ace_pa_s_kernel(tc, h_enc, enc_w2, enc_b2, clus_w, clus_b, z_out, conf_
             out=h_grouped[:].bitcast(F32).rearrange("q (g b u) -> q g b u", g=HIDDEN_PASSES, u=2),
             in_=h_wordsT[:].rearrange("q g u b -> q g b u"),
         )
+        b2 = keep.tile([P, PACK], F32)
+        nc.vector.tensor_copy(out=b2[:], in_=b2_bf16[:])
         h_codes = keep.tile([P, HIDDEN_PASSES * P], U32, align_bytes=64)
         h_scales = keep.tile([P, HIDDEN_PASSES * P], U8, align_bytes=64)
         nc.vector.quantize_mx(out=h_codes[:].bitcast(FP8X4), scales=h_scales[:], in_=h_grouped[:])
@@ -146,6 +146,9 @@ def tile_ace_pa_s_kernel(tc, h_enc, enc_w2, enc_b2, clus_w, clus_b, z_out, conf_
 
         def by_module(columns):
             return columns.rearrange("b (r m i) -> b m r i", r=ROWS_PER_PARTITION, m=CHUNK_MODULES)
+
+        def by_row(columns):
+            return columns.rearrange("b (r m i) -> b r m i", r=ROWS_PER_PARTITION, m=CHUNK_MODULES)
 
         def transpose_chunk(j):
             words = cw_rows[j][:].bitcast(F32)
@@ -179,16 +182,25 @@ def tile_ace_pa_s_kernel(tc, h_enc, enc_w2, enc_b2, clus_w, clus_b, z_out, conf_
                 start=True,
                 stop=True,
             )
-            nc.vector.scalar_tensor_tensor(
-                out=scaled[j][:], in0=sums[:], scalar=-BETA, in1=bias_rows[j][:], op0=ALU.mult, op1=ALU.add
-            )
-            nc.vector.tensor_reduce(
-                out=neg_max[:, j * CHUNK_MODULES : (j + 1) * CHUNK_MODULES],
-                in_=by_module(scaled[j][:]),
-                axis=AXIS.XY,
-                op=ALU.max,
-                negate=True,
-            )
+            for first in range(0, CHUNK_MODULES, GROUP_MODULES):
+                group = slice(first, first + GROUP_MODULES)
+                nc.vector.scalar_tensor_tensor(
+                    out=by_row(scaled[j][:])[:, :, group, :].rearrange("b r m i -> b r (m i)"),
+                    in0=by_row(sums[:])[:, :, group, :].rearrange("b r m i -> b r (m i)"),
+                    scalar=-BETA,
+                    in1=by_row(bias_rows[j][:])[:, :, group, :].rearrange("b r m i -> b r (m i)"),
+                    op0=ALU.mult,
+                    op1=ALU.add,
+                )
+            for first in range(0, CHUNK_MODULES, GROUP_MODULES):
+                c = j * CHUNK_MODULES + first
+                nc.vector.tensor_reduce(
+                    out=neg_max[:, c : c + GROUP_MODULES],
+                    in_=by_module(scaled[j][:])[:, first : first + GROUP_MODULES, :, :],
+                    axis=AXIS.XY,
+                    op=ALU.max,
+                    negate=True,
+                )
 
         def sum_exps_chunk(j):
             exps = keep.tile([P, CHUNK_ROWS], F32, name="exps%d" % j)
@@ -218,7 +230,6 @@ def tile_ace_pa_s_kernel(tc, h_enc, enc_w2, enc_b2, clus_w, clus_b, z_out, conf_
                 )
 
         transpose_chunk(1)
-        quantise_chunk(0)
 
         z_grouped = keep.tile([P, P * PACK], BF16, align_bytes=64)
         nc.vector.tensor_tensor(
@@ -227,6 +238,7 @@ def tile_ace_pa_s_kernel(tc, h_enc, enc_w2, enc_b2, clus_w, clus_b, z_out, conf_
             in1=b2[:].unsqueeze(1).to_broadcast([P, P, PACK]),
             op=ALU.add,
         )
+        quantise_chunk(0)
         z_codes = keep.tile([P, P], U32, align_bytes=64)
         z_scales = keep.tile([P, P], U8, align_bytes=64)
         nc.vector.quantize_mx(out=z_codes[:].bitcast(FP8X4), scales=z_scales[:], in_=z_grouped[:])

@@ -23,11 +23,11 @@ BETA = 10.0
 
 HIDDEN_PASSES = HIDDEN // K_PASS
 LATENT_TILES = LATENT // P
-CHUNK_ROWS = 512
+CHUNK_ROWS = 256
 CHUNKS = MODULES * HEADS // CHUNK_ROWS
 ROWS_PER_PARTITION = CHUNK_ROWS // P
 CHUNK_MODULES = CHUNK_ROWS // HEADS
-GROUP_MODULES = CHUNK_MODULES // 2
+AHEAD = 4
 
 FLOPS = 2 * P * HIDDEN * LATENT + 2 * P * LATENT * MODULES * HEADS
 
@@ -38,7 +38,6 @@ def tile_ace_pa_s_kernel(tc, h_enc, enc_w2, enc_b2, clus_w, clus_b, z_out, conf_
         keep = stack.enter_context(tc.tile_pool(name="keep", bufs=1))
         psum_t = stack.enter_context(tc.psum_pool(name="psum_t", bufs=4))
         psum_mx = stack.enter_context(tc.psum_pool(name="psum_mx", bufs=4))
-        stack.enter_context(tc.manual_schedule())
 
         cb_bf16 = keep.tile([P, CHUNKS, ROWS_PER_PARTITION], BF16)
         nc.sync.dma_start(
@@ -85,16 +84,18 @@ def tile_ace_pa_s_kernel(tc, h_enc, enc_w2, enc_b2, clus_w, clus_b, z_out, conf_
 
         cb_scaled = keep.tile([P, CHUNKS, ROWS_PER_PARTITION], F32)
         nc.vector.tensor_scalar_mul(out=cb_scaled[:], in0=cb_bf16[:], scalar1=-BETA)
-        bias_rows = []
-        for j in range(CHUNKS):
-            spread = psum_t.tile([P, ROWS_PER_PARTITION, P], F32, tag="t")
-            for r in range(ROWS_PER_PARTITION):
+        cb_columns = cb_scaled[:].rearrange("p j r -> p (j r)")
+        bias_rows = keep.tile([P, CHUNKS, CHUNK_ROWS], F32)
+        bias_banks = bias_rows[:].rearrange("b j c -> b (j c)")
+        for first in range(0, CHUNKS * ROWS_PER_PARTITION, 4):
+            spread = psum_t.tile([P, 4, P], F32, tag="t")
+            for i in range(4):
                 nc.tensor.transpose(
-                    spread[:, r, :], cb_scaled[:, j, r : r + 1].to_broadcast([P, P]), identity[:]
+                    spread[:, i, :], cb_columns[:, first + i : first + i + 1].to_broadcast([P, P]), identity[:]
                 )
-            rows = keep.tile([P, CHUNK_ROWS], F32, name="bias_rows%d" % j)
-            nc.scalar.copy(out=rows[:], in_=spread[:].rearrange("b r p -> b (r p)"))
-            bias_rows.append(rows)
+            nc.scalar.copy(
+                out=bias_banks[:, first * P : (first + 4) * P], in_=spread[:].rearrange("b i p -> b (i p)")
+            )
 
         w2_grouped = []
         for g in range(HIDDEN_PASSES):
@@ -147,24 +148,17 @@ def tile_ace_pa_s_kernel(tc, h_enc, enc_w2, enc_b2, clus_w, clus_b, z_out, conf_
         def by_module(columns):
             return columns.rearrange("b (r m i) -> b m r i", r=ROWS_PER_PARTITION, m=CHUNK_MODULES)
 
-        def by_row(columns):
-            return columns.rearrange("b (r m i) -> b r m i", r=ROWS_PER_PARTITION, m=CHUNK_MODULES)
-
         def transpose_chunk(j):
             words = cw_rows[j][:].bitcast(F32)
-            grouped_words = cw_grouped[j][:].bitcast(F32).rearrange(
-                "q (r p u) -> q r p u", r=ROWS_PER_PARTITION, u=2
+            wordsT = psum_t.tile([P, ROWS_PER_PARTITION, 2, P], F32, tag="t")
+            for r in range(ROWS_PER_PARTITION):
+                for u in range(2):
+                    first = (r * 2 + u) * P
+                    nc.tensor.transpose(wordsT[:, r, u, :], words[:, first : first + P], identity[:])
+            nc.scalar.copy(
+                out=cw_grouped[j][:].bitcast(F32).rearrange("q (r p u) -> q r p u", r=ROWS_PER_PARTITION, u=2),
+                in_=wordsT[:].rearrange("q r u p -> q r p u"),
             )
-            for half in range(2):
-                wordsT = psum_t.tile([P, 2, 2, P], F32, tag="t")
-                for r in range(2):
-                    for u in range(2):
-                        first = ((2 * half + r) * 2 + u) * P
-                        nc.tensor.transpose(wordsT[:, r, u, :], words[:, first : first + P], identity[:])
-                nc.scalar.copy(
-                    out=grouped_words[:, 2 * half : 2 * half + 2, :, :],
-                    in_=wordsT[:].rearrange("q r u p -> q r p u"),
-                )
 
         def quantise_chunk(j):
             nc.vector.quantize_mx(
@@ -182,25 +176,18 @@ def tile_ace_pa_s_kernel(tc, h_enc, enc_w2, enc_b2, clus_w, clus_b, z_out, conf_
                 start=True,
                 stop=True,
             )
-            for first in range(0, CHUNK_MODULES, GROUP_MODULES):
-                group = slice(first, first + GROUP_MODULES)
-                nc.vector.scalar_tensor_tensor(
-                    out=by_row(scaled[j][:])[:, :, group, :].rearrange("b r m i -> b r (m i)"),
-                    in0=by_row(sums[:])[:, :, group, :].rearrange("b r m i -> b r (m i)"),
-                    scalar=-BETA,
-                    in1=by_row(bias_rows[j][:])[:, :, group, :].rearrange("b r m i -> b r (m i)"),
-                    op0=ALU.mult,
-                    op1=ALU.add,
-                )
-            for first in range(0, CHUNK_MODULES, GROUP_MODULES):
-                c = j * CHUNK_MODULES + first
-                nc.vector.tensor_reduce(
-                    out=neg_max[:, c : c + GROUP_MODULES],
-                    in_=by_module(scaled[j][:])[:, first : first + GROUP_MODULES, :, :],
-                    axis=AXIS.XY,
-                    op=ALU.max,
-                    negate=True,
-                )
+            nc.vector.scalar_tensor_tensor(
+                out=scaled[j][:], in0=sums[:], scalar=-BETA, in1=bias_rows[:, j, :], op0=ALU.mult, op1=ALU.add
+            )
+
+        def max_chunk(j):
+            nc.vector.tensor_reduce(
+                out=neg_max[:, j * CHUNK_MODULES : (j + 1) * CHUNK_MODULES],
+                in_=by_module(scaled[j][:]),
+                axis=AXIS.XY,
+                op=ALU.max,
+                negate=True,
+            )
 
         def sum_exps_chunk(j):
             exps = keep.tile([P, CHUNK_ROWS], F32, name="exps%d" % j)
@@ -215,6 +202,7 @@ def tile_ace_pa_s_kernel(tc, h_enc, enc_w2, enc_b2, clus_w, clus_b, z_out, conf_
                 )
 
         transpose_chunk(0)
+        transpose_chunk(1)
 
         zT_sums = psum_mx.tile([P, LATENT_TILES, P], F32, tag="mx")
         for t in range(LATENT_TILES):
@@ -229,7 +217,8 @@ def tile_ace_pa_s_kernel(tc, h_enc, enc_w2, enc_b2, clus_w, clus_b, z_out, conf_
                     stop=(g == HIDDEN_PASSES - 1),
                 )
 
-        transpose_chunk(1)
+        transpose_chunk(2)
+        transpose_chunk(3)
 
         z_grouped = keep.tile([P, P * PACK], BF16, align_bytes=64)
         nc.vector.tensor_tensor(
@@ -242,7 +231,8 @@ def tile_ace_pa_s_kernel(tc, h_enc, enc_w2, enc_b2, clus_w, clus_b, z_out, conf_
         z_codes = keep.tile([P, P], U32, align_bytes=64)
         z_scales = keep.tile([P, P], U8, align_bytes=64)
         nc.vector.quantize_mx(out=z_codes[:].bitcast(FP8X4), scales=z_scales[:], in_=z_grouped[:])
-        quantise_chunk(1)
+        for j in range(1, AHEAD):
+            quantise_chunk(j)
 
         zT = keep.tile([P, LATENT_TILES, P], F32)
         for t in range(LATENT_TILES):
@@ -250,15 +240,18 @@ def tile_ace_pa_s_kernel(tc, h_enc, enc_w2, enc_b2, clus_w, clus_b, z_out, conf_
                 out=zT[:, t, :], in_=zT_sums[:, t, :], func=ACT.Identity, bias=b2[:, t : t + 1]
             )
 
-        for j in range(CHUNKS):
-            if j + 2 < CHUNKS:
-                transpose_chunk(j + 2)
-            score_chunk(j)
-            if j + 2 < CHUNKS:
-                quantise_chunk(j + 2)
-            if j >= 1:
-                sum_exps_chunk(j - 1)
-            if j == 1:
+        for j in range(CHUNKS + 2):
+            if j + AHEAD < CHUNKS:
+                transpose_chunk(j + AHEAD)
+            if j < CHUNKS:
+                score_chunk(j)
+            if 1 <= j <= CHUNKS:
+                max_chunk(j - 1)
+            if j + AHEAD < CHUNKS:
+                quantise_chunk(j + AHEAD)
+            if j >= 2:
+                sum_exps_chunk(j - 2)
+            if j == 3:
                 z_tiles = psum_t.tile([P, LATENT_TILES, P], F32, tag="t")
                 for t in range(LATENT_TILES):
                     nc.tensor.transpose(z_tiles[:, t, :], zT[:, t, :], identity[:])
@@ -268,7 +261,6 @@ def tile_ace_pa_s_kernel(tc, h_enc, enc_w2, enc_b2, clus_w, clus_b, z_out, conf_
                     in_=z_tiles[:].rearrange("b (u e) q -> b u q e", e=2),
                 )
                 nc.sync.dma_start(out=z_out, in_=z_rows[:])
-        sum_exps_chunk(CHUNKS - 1)
 
         log_sum = keep.tile([P, MODULES], F32)
         nc.scalar.activation(out=log_sum[:], in_=exp_sum[:], func=ACT.Ln)

@@ -23,11 +23,11 @@ BETA = 10.0
 
 HIDDEN_PASSES = HIDDEN // K_PASS
 LATENT_TILES = LATENT // P
-CHUNK_ROWS = 256
+CHUNK_ROWS = 512
 CHUNKS = MODULES * HEADS // CHUNK_ROWS
 ROWS_PER_PARTITION = CHUNK_ROWS // P
 CHUNK_MODULES = CHUNK_ROWS // HEADS
-AHEAD = 4
+GROUP_MODULES = CHUNK_MODULES // 2
 
 FLOPS = 2 * P * HIDDEN * LATENT + 2 * P * LATENT * MODULES * HEADS
 
@@ -84,18 +84,16 @@ def tile_ace_pa_s_kernel(tc, h_enc, enc_w2, enc_b2, clus_w, clus_b, z_out, conf_
 
         cb_scaled = keep.tile([P, CHUNKS, ROWS_PER_PARTITION], F32)
         nc.vector.tensor_scalar_mul(out=cb_scaled[:], in0=cb_bf16[:], scalar1=-BETA)
-        cb_columns = cb_scaled[:].rearrange("p j r -> p (j r)")
-        bias_rows = keep.tile([P, CHUNKS, CHUNK_ROWS], F32)
-        bias_banks = bias_rows[:].rearrange("b j c -> b (j c)")
-        for first in range(0, CHUNKS * ROWS_PER_PARTITION, 4):
-            spread = psum_t.tile([P, 4, P], F32, tag="t")
-            for i in range(4):
+        bias_rows = []
+        for j in range(CHUNKS):
+            spread = psum_t.tile([P, ROWS_PER_PARTITION, P], F32, tag="t")
+            for r in range(ROWS_PER_PARTITION):
                 nc.tensor.transpose(
-                    spread[:, i, :], cb_columns[:, first + i : first + i + 1].to_broadcast([P, P]), identity[:]
+                    spread[:, r, :], cb_scaled[:, j, r : r + 1].to_broadcast([P, P]), identity[:]
                 )
-            nc.scalar.copy(
-                out=bias_banks[:, first * P : (first + 4) * P], in_=spread[:].rearrange("b i p -> b (i p)")
-            )
+            rows = keep.tile([P, CHUNK_ROWS], F32, name="bias_rows%d" % j)
+            nc.scalar.copy(out=rows[:], in_=spread[:].rearrange("b r p -> b (r p)"))
+            bias_rows.append(rows)
 
         w2_grouped = []
         for g in range(HIDDEN_PASSES):
@@ -148,17 +146,24 @@ def tile_ace_pa_s_kernel(tc, h_enc, enc_w2, enc_b2, clus_w, clus_b, z_out, conf_
         def by_module(columns):
             return columns.rearrange("b (r m i) -> b m r i", r=ROWS_PER_PARTITION, m=CHUNK_MODULES)
 
+        def by_row(columns):
+            return columns.rearrange("b (r m i) -> b r m i", r=ROWS_PER_PARTITION, m=CHUNK_MODULES)
+
         def transpose_chunk(j):
             words = cw_rows[j][:].bitcast(F32)
-            wordsT = psum_t.tile([P, ROWS_PER_PARTITION, 2, P], F32, tag="t")
-            for r in range(ROWS_PER_PARTITION):
-                for u in range(2):
-                    first = (r * 2 + u) * P
-                    nc.tensor.transpose(wordsT[:, r, u, :], words[:, first : first + P], identity[:])
-            nc.scalar.copy(
-                out=cw_grouped[j][:].bitcast(F32).rearrange("q (r p u) -> q r p u", r=ROWS_PER_PARTITION, u=2),
-                in_=wordsT[:].rearrange("q r u p -> q r p u"),
+            grouped_words = cw_grouped[j][:].bitcast(F32).rearrange(
+                "q (r p u) -> q r p u", r=ROWS_PER_PARTITION, u=2
             )
+            for half in range(2):
+                wordsT = psum_t.tile([P, 2, 2, P], F32, tag="t")
+                for r in range(2):
+                    for u in range(2):
+                        first = ((2 * half + r) * 2 + u) * P
+                        nc.tensor.transpose(wordsT[:, r, u, :], words[:, first : first + P], identity[:])
+                nc.scalar.copy(
+                    out=grouped_words[:, 2 * half : 2 * half + 2, :, :],
+                    in_=wordsT[:].rearrange("q r u p -> q r p u"),
+                )
 
         def quantise_chunk(j):
             nc.vector.quantize_mx(
@@ -176,18 +181,25 @@ def tile_ace_pa_s_kernel(tc, h_enc, enc_w2, enc_b2, clus_w, clus_b, z_out, conf_
                 start=True,
                 stop=True,
             )
-            nc.vector.scalar_tensor_tensor(
-                out=scaled[j][:], in0=sums[:], scalar=-BETA, in1=bias_rows[:, j, :], op0=ALU.mult, op1=ALU.add
-            )
-
-        def max_chunk(j):
-            nc.vector.tensor_reduce(
-                out=neg_max[:, j * CHUNK_MODULES : (j + 1) * CHUNK_MODULES],
-                in_=by_module(scaled[j][:]),
-                axis=AXIS.XY,
-                op=ALU.max,
-                negate=True,
-            )
+            for first in range(0, CHUNK_MODULES, GROUP_MODULES):
+                group = slice(first, first + GROUP_MODULES)
+                nc.vector.scalar_tensor_tensor(
+                    out=by_row(scaled[j][:])[:, :, group, :].rearrange("b r m i -> b r (m i)"),
+                    in0=by_row(sums[:])[:, :, group, :].rearrange("b r m i -> b r (m i)"),
+                    scalar=-BETA,
+                    in1=by_row(bias_rows[j][:])[:, :, group, :].rearrange("b r m i -> b r (m i)"),
+                    op0=ALU.mult,
+                    op1=ALU.add,
+                )
+            for first in range(0, CHUNK_MODULES, GROUP_MODULES):
+                c = j * CHUNK_MODULES + first
+                nc.vector.tensor_reduce(
+                    out=neg_max[:, c : c + GROUP_MODULES],
+                    in_=by_module(scaled[j][:])[:, first : first + GROUP_MODULES, :, :],
+                    axis=AXIS.XY,
+                    op=ALU.max,
+                    negate=True,
+                )
 
         def sum_exps_chunk(j):
             exps = keep.tile([P, CHUNK_ROWS], F32, name="exps%d" % j)
@@ -202,7 +214,6 @@ def tile_ace_pa_s_kernel(tc, h_enc, enc_w2, enc_b2, clus_w, clus_b, z_out, conf_
                 )
 
         transpose_chunk(0)
-        transpose_chunk(1)
 
         zT_sums = psum_mx.tile([P, LATENT_TILES, P], F32, tag="mx")
         for t in range(LATENT_TILES):
@@ -217,8 +228,7 @@ def tile_ace_pa_s_kernel(tc, h_enc, enc_w2, enc_b2, clus_w, clus_b, z_out, conf_
                     stop=(g == HIDDEN_PASSES - 1),
                 )
 
-        transpose_chunk(2)
-        transpose_chunk(3)
+        transpose_chunk(1)
 
         z_grouped = keep.tile([P, P * PACK], BF16, align_bytes=64)
         nc.vector.tensor_tensor(
@@ -231,8 +241,7 @@ def tile_ace_pa_s_kernel(tc, h_enc, enc_w2, enc_b2, clus_w, clus_b, z_out, conf_
         z_codes = keep.tile([P, P], U32, align_bytes=64)
         z_scales = keep.tile([P, P], U8, align_bytes=64)
         nc.vector.quantize_mx(out=z_codes[:].bitcast(FP8X4), scales=z_scales[:], in_=z_grouped[:])
-        for j in range(1, AHEAD):
-            quantise_chunk(j)
+        quantise_chunk(1)
 
         zT = keep.tile([P, LATENT_TILES, P], F32)
         for t in range(LATENT_TILES):
@@ -240,18 +249,15 @@ def tile_ace_pa_s_kernel(tc, h_enc, enc_w2, enc_b2, clus_w, clus_b, z_out, conf_
                 out=zT[:, t, :], in_=zT_sums[:, t, :], func=ACT.Identity, bias=b2[:, t : t + 1]
             )
 
-        for j in range(CHUNKS + 2):
-            if j + AHEAD < CHUNKS:
-                transpose_chunk(j + AHEAD)
-            if j < CHUNKS:
-                score_chunk(j)
-            if 1 <= j <= CHUNKS:
-                max_chunk(j - 1)
-            if j + AHEAD < CHUNKS:
-                quantise_chunk(j + AHEAD)
-            if j >= 2:
-                sum_exps_chunk(j - 2)
-            if j == 3:
+        for j in range(CHUNKS):
+            if j + 2 < CHUNKS:
+                transpose_chunk(j + 2)
+            score_chunk(j)
+            if j + 2 < CHUNKS:
+                quantise_chunk(j + 2)
+            if j >= 1:
+                sum_exps_chunk(j - 1)
+            if j == 1:
                 z_tiles = psum_t.tile([P, LATENT_TILES, P], F32, tag="t")
                 for t in range(LATENT_TILES):
                     nc.tensor.transpose(z_tiles[:, t, :], zT[:, t, :], identity[:])
@@ -261,6 +267,7 @@ def tile_ace_pa_s_kernel(tc, h_enc, enc_w2, enc_b2, clus_w, clus_b, z_out, conf_
                     in_=z_tiles[:].rearrange("b (u e) q -> b u q e", e=2),
                 )
                 nc.sync.dma_start(out=z_out, in_=z_rows[:])
+        sum_exps_chunk(CHUNKS - 1)
 
         log_sum = keep.tile([P, MODULES], F32)
         nc.scalar.activation(out=log_sum[:], in_=exp_sum[:], func=ACT.Ln)

from contextlib import ExitStack

import concourse.mybir as mybir
from concourse.masks import make_identity

F32 = mybir.dt.float32
BF16 = mybir.dt.bfloat16
U32 = mybir.dt.uint32
U8 = mybir.dt.uint8
FP8X4 = mybir.dt.float8_e4m3fn_x4
ALU = mybir.AluOpType
ACT = mybir.ActivationFunctionType
AXIS = mybir.AxisListType

P = 128
PACK = 4
K_PASS = P * PACK
HIDDEN = 1024
LATENT = 512
MODULES = 32
HEADS = 64
BETA = 10.0

HIDDEN_PASSES = HIDDEN // K_PASS
LATENT_TILES = LATENT // P
CHUNK_ROWS = 512
CHUNKS = MODULES * HEADS // CHUNK_ROWS
ROWS_PER_PARTITION = CHUNK_ROWS // P
CHUNK_MODULES = CHUNK_ROWS // HEADS
GROUP_MODULES = CHUNK_MODULES // 2

FLOPS = 2 * P * HIDDEN * LATENT + 2 * P * LATENT * MODULES * HEADS


def tile_ace_pa_s_kernel(tc, h_enc, enc_w2, enc_b2, clus_w, clus_b, z_out, conf_out):
    nc = tc.nc
    with ExitStack() as stack:
        keep = stack.enter_context(tc.tile_pool(name="keep", bufs=1))
        psum_t = stack.enter_context(tc.psum_pool(name="psum_t", bufs=4))
        psum_mx = stack.enter_context(tc.psum_pool(name="psum_mx", bufs=4))

        cb_bf16 = keep.tile([P, CHUNKS, ROWS_PER_PARTITION], BF16)
        nc.sync.dma_start(
            out=cb_bf16[:],
            in_=clus_b.rearrange("c k -> (c k)").rearrange(
                "(j p r) -> p j r", j=CHUNKS, r=ROWS_PER_PARTITION
            ),
        )
        w2_rows = []
        for g in range(HIDDEN_PASSES):
            rows = keep.tile([P, PACK, LATENT], BF16, name="w2_rows%d" % g)
            nc.sync.dma_start(
                out=rows[:].rearrange("q (u e) d -> q u (e d)", e=2),
                in_=enc_w2[g * K_PASS : (g + 1) * K_PASS, :].rearrange(
                    "(u q e) d -> q u (e d)", u=2, e=2
                ),
            )
            w2_rows.append(rows)
        h_rows = keep.tile([P, HIDDEN], BF16)
        nc.sync.dma_start(out=h_rows[:], in_=h_enc)
        b2_bf16 = keep.tile([P, PACK], BF16)
        nc.sync.dma_start(
            out=b2_bf16[:].rearrange("q (u e) -> q u e", e=2),
            in_=enc_b2.rearrange("(u q e) -> q u e", u=2, e=2),
        )
        clus_w_rows = clus_w.rearrange("c k d -> (c k) d")
        cw_rows = []
        for j in range(CHUNKS):
            rows = keep.tile([P, ROWS_PER_PARTITION * LATENT], BF16, name="cw_rows%d" % j)
            nc.sync.dma_start(
                out=rows[:],
                in_=clus_w_rows[j * CHUNK_ROWS : (j + 1) * CHUNK_ROWS, :].rearrange(
                    "(p r) d -> p (r d)", r=ROWS_PER_PARTITION
                ),
            )
            cw_rows.append(rows)

        identity = keep.tile([P, P], F32)
        make_identity(nc, identity[:])
        one_column = keep.tile([P, 1], F32)
        nc.vector.memset(one_column[:], 0.0)
        table_warmer = keep.tile([P, 1], F32)
        nc.scalar.activation(out=table_warmer[:], in_=one_column[:], func=ACT.Exp)

        cb_scaled = keep.tile([P, CHUNKS, ROWS_PER_PARTITION], F32)
        nc.vector.tensor_scalar_mul(out=cb_scaled[:], in0=cb_bf16[:], scalar1=-BETA)
        bias_rows = []
        for j in range(CHUNKS):
            spread = psum_t.tile([P, ROWS_PER_PARTITION, P], F32, tag="t")
            for r in range(ROWS_PER_PARTITION):
                nc.tensor.transpose(
                    spread[:, r, :], cb_scaled[:, j, r : r + 1].to_broadcast([P, P]), identity[:]
                )
            rows = keep.tile([P, CHUNK_ROWS], F32, name="bias_rows%d" % j)
            nc.scalar.copy(out=rows[:], in_=spread[:].rearrange("b r p -> b (r p)"))
            bias_rows.append(rows)

        w2_grouped = []
        for g in range(HIDDEN_PASSES):
            grouped = keep.tile([P, LATENT * PACK], BF16, align_bytes=64, name="w2_grouped%d" % g)
            nc.vector.tensor_copy(
                out=grouped[:].rearrange("p (u e q t) -> p u e q t", u=2, e=2, t=PACK),
                in_=w2_rows[g][:].rearrange("p t (u q e) -> p u e q t", u=2, e=2),
            )
            w2_grouped.append(grouped)
        w2_codes = []
        w2_scales = []
        for g in range(HIDDEN_PASSES):
            codes = keep.tile([P, LATENT], U32, align_bytes=64, name="w2_codes%d" % g)
            scales = keep.tile([P, LATENT], U8, align_bytes=64, name="w2_scales%d" % g)
            nc.vector.quantize_mx(out=codes[:].bitcast(FP8X4), scales=scales[:], in_=w2_grouped[g][:])
            w2_codes.append(codes)
            w2_scales.append(scales)

        h_words = h_rows[:].bitcast(F32)
        h_wordsT = psum_t.tile([P, HIDDEN_PASSES, 2, P], F32, tag="t")
        for g in range(HIDDEN_PASSES):
            for u in range(2):
                first = (2 * g + u) * P
                nc.tensor.transpose(h_wordsT[:, g, u, :], h_words[:, first : first + P], identity[:])
        h_grouped = keep.tile([P, HIDDEN_PASSES * P * PACK], BF16, align_bytes=64)
        nc.scalar.copy(
            out=h_grouped[:].bitcast(F32).rearrange("q (g b u) -> q g b u", g=HIDDEN_PASSES, u=2),
            in_=h_wordsT[:].rearrange("q g u b -> q g b u"),
        )
        b2 = keep.tile([P, PACK], F32)
        nc.vector.tensor_copy(out=b2[:], in_=b2_bf16[:])
        h_codes = keep.tile([P, HIDDEN_PASSES * P], U32, align_bytes=64)
        h_scales = keep.tile([P, HIDDEN_PASSES * P], U8, align_bytes=64)
        nc.vector.quantize_mx(out=h_codes[:].bitcast(FP8X4), scales=h_scales[:], in_=h_grouped[:])

        cw_grouped = [
            keep.tile([P, CHUNK_ROWS * PACK], BF16, align_bytes=64, name="cw_grouped%d" % j)
            for j in range(CHUNKS)
        ]
        cw_codes = [
            keep.tile([P, CHUNK_ROWS], U32, align_bytes=64, name="cw_codes%d" % j) for j in range(CHUNKS)
        ]
        cw_scales = [
            keep.tile([P, CHUNK_ROWS], U8, align_bytes=64, name="cw_scales%d" % j) for j in range(CHUNKS)
        ]
        scaled = [keep.tile([P, CHUNK_ROWS], F32, name="scaled%d" % j) for j in range(CHUNKS)]
        neg_max = keep.tile([P, MODULES], F32)
        exp_sum = keep.tile([P, MODULES], F32)

        def by_module(columns):
            return columns.rearrange("b (r m i) -> b m r i", r=ROWS_PER_PARTITION, m=CHUNK_MODULES)

        def by_row(columns):
            return columns.rearrange("b (r m i) -> b r m i", r=ROWS_PER_PARTITION, m=CHUNK_MODULES)

        def transpose_chunk(j):
            words = cw_rows[j][:].bitcast(F32)
            grouped_words = cw_grouped[j][:].bitcast(F32).rearrange(
                "q (r p u) -> q r p u", r=ROWS_PER_PARTITION, u=2
            )
            for half in range(2):
                wordsT = psum_t.tile([P, 2, 2, P], F32, tag="t")
                for r in range(2):
                    for u in range(2):
                        first = ((2 * half + r) * 2 + u) * P
                        nc.tensor.transpose(wordsT[:, r, u, :], words[:, first : first + P], identity[:])
                nc.scalar.copy(
                    out=grouped_words[:, 2 * half : 2 * half + 2, :, :],
                    in_=wordsT[:].rearrange("q r u p -> q r p u"),
                )

        def quantise_chunk(j):
            nc.vector.quantize_mx(
                out=cw_codes[j][:].bitcast(FP8X4), scales=cw_scales[j][:], in_=cw_grouped[j][:]
            )

        def score_chunk(j):
            sums = psum_mx.tile([P, CHUNK_ROWS], F32, tag="mx")
            nc.tensor.matmul_mx(
                out=sums[:],
                lhsT=z_codes[:].bitcast(FP8X4),
                lhsT_scale=z_scales[:],
                rhs=cw_codes[j][:].bitcast(FP8X4),
                rhs_scale=cw_scales[j][:],
                start=True,
                stop=True,
            )
            for first in range(0, CHUNK_MODULES, GROUP_MODULES):
                group = slice(first, first + GROUP_MODULES)
                nc.vector.scalar_tensor_tensor(
                    out=by_row(scaled[j][:])[:, :, group, :].rearrange("b r m i -> b r (m i)"),
                    in0=by_row(sums[:])[:, :, group, :].rearrange("b r m i -> b r (m i)"),
                    scalar=-BETA,
                    in1=by_row(bias_rows[j][:])[:, :, group, :].rearrange("b r m i -> b r (m i)"),
                    op0=ALU.mult,
                    op1=ALU.add,
                )
            for first in range(0, CHUNK_MODULES, GROUP_MODULES):
                c = j * CHUNK_MODULES + first
                nc.vector.tensor_reduce(
                    out=neg_max[:, c : c + GROUP_MODULES],
                    in_=by_module(scaled[j][:])[:, first : first + GROUP_MODULES, :, :],
                    axis=AXIS.XY,
                    op=ALU.max,
                    negate=True,
                )

        def sum_exps_chunk(j):
            exps = keep.tile([P, CHUNK_ROWS], F32, name="exps%d" % j)
            for m in range(CHUNK_MODULES):
                c = j * CHUNK_MODULES + m
                nc.scalar.activation(
                    out=by_module(exps[:])[:, m, :, :],
                    in_=by_module(scaled[j][:])[:, m, :, :],
                    func=ACT.Exp,
                    bias=neg_max[:, c : c + 1],
                    accum_out=exp_sum[:, c : c + 1],
                )

        transpose_chunk(0)

        zT_sums = psum_mx.tile([P, LATENT_TILES, P], F32, tag="mx")
        for t in range(LATENT_TILES):
            for g in range(HIDDEN_PASSES):
                nc.tensor.matmul_mx(
                    out=zT_sums[:, t, :],
                    lhsT=w2_codes[g][:, t * P : (t + 1) * P].bitcast(FP8X4),
                    lhsT_scale=w2_scales[g][:, t * P : (t + 1) * P],
                    rhs=h_codes[:, g * P : (g + 1) * P].bitcast(FP8X4),
                    rhs_scale=h_scales[:, g * P : (g + 1) * P],
                    start=(g == 0),
                    stop=(g == HIDDEN_PASSES - 1),
                )

        transpose_chunk(1)

        z_grouped = keep.tile([P, P * PACK], BF16, align_bytes=64)
        nc.vector.tensor_tensor(
            out=z_grouped[:].rearrange("q (b t) -> q b t", t=PACK),
            in0=zT_sums[:].rearrange("q t b -> q b t"),
            in1=b2[:].unsqueeze(1).to_broadcast([P, P, PACK]),
            op=ALU.add,
        )
        quantise_chunk(0)
        z_codes = keep.tile([P, P], U32, align_bytes=64)
        z_scales = keep.tile([P, P], U8, align_bytes=64)
        nc.vector.quantize_mx(out=z_codes[:].bitcast(FP8X4), scales=z_scales[:], in_=z_grouped[:])
        quantise_chunk(1)

        zT = keep.tile([P, LATENT_TILES, P], F32)
        for t in range(LATENT_TILES):
            nc.scalar.activation(
                out=zT[:, t, :], in_=zT_sums[:, t, :], func=ACT.Identity, bias=b2[:, t : t + 1]
            )

        for j in range(CHUNKS):
            if j + 2 < CHUNKS:
                transpose_chunk(j + 2)
            score_chunk(j)
            if j + 2 < CHUNKS:
                quantise_chunk(j + 2)
            if j >= 1:
                sum_exps_chunk(j - 1)
            if j == 1:
                z_tiles = psum_t.tile([P, LATENT_TILES, P], F32, tag="t")
                for t in range(LATENT_TILES):
                    nc.tensor.transpose(z_tiles[:, t, :], zT[:, t, :], identity[:])
                z_rows = keep.tile([P, LATENT], F32)
                nc.scalar.copy(
                    out=z_rows[:].rearrange("b (u q e) -> b u q e", u=2, e=2),
                    in_=z_tiles[:].rearrange("b (u e) q -> b u q e", e=2),
                )
                nc.sync.dma_start(out=z_out, in_=z_rows[:])
        sum_exps_chunk(CHUNKS - 1)

        log_sum = keep.tile([P, MODULES], F32)
        nc.scalar.activation(out=log_sum[:], in_=exp_sum[:], func=ACT.Ln)
        conf = keep.tile([P, MODULES], F32)
        nc.vector.tensor_sub(out=conf[:], in0=neg_max[:], in1=log_sum[:])
        nc.sync.dma_start(out=conf_out, in_=conf[:])
